import numpy as np
import ml_dtypes


def mxq(x, axis, fmt="e4m3"):
    dtype, down = {"e4m3": (ml_dtypes.float8_e4m3fn, 7), "e5m2": (ml_dtypes.float8_e5m2, 14)}[fmt]
    v = np.moveaxis(np.asarray(x, np.float32).astype(ml_dtypes.bfloat16).astype(np.float64), axis, -1)
    blocks = v.reshape(v.shape[:-1] + (-1, 32))
    amax = np.abs(blocks).max(-1, keepdims=True)
    byte = np.maximum(np.where(amax > 0, np.frexp(amax)[1] - 1 + 127, 0) - down, 1)
    scale = np.exp2(byte - 127.0)
    codes = (blocks / scale).astype(np.float32).astype(dtype).astype(np.float64)
    return np.moveaxis((codes * scale).reshape(v.shape), -1, axis)


WIDE = False


def mx_kscale(k):
    if not WIDE:
        return np.ones(k)
    levels = np.array([10, -10, 5, -5, 0])
    if k % 512:
        return np.exp2(np.random.permutation(np.resize(levels, k // 32))).repeat(32)
    a = np.empty((k // 512, 16))
    for p in range(k // 512):
        a[p, :8] = np.random.permutation(np.resize(levels, 8))
        for g in range(8):
            far = levels[np.abs(levels - a[p, g]) >= 10]
            a[p, g + 8] = far[np.random.randint(len(far))]
    return np.exp2(a.ravel()).repeat(32)


BF16 = ml_dtypes.bfloat16


def bf(x):
    return np.asarray(x, np.float32).astype(BF16)


def f64(x):
    return np.asarray(x).astype(np.float64)


B, D, DO, H, T, P = 128, 1024, 1024, 256, 8, 2


def setup_inputs():
    s = mx_kscale(D)
    return {"transformed": bf(np.random.standard_normal((B, D)) * 1.2 * s),
            "coeff": bf(np.random.standard_normal((B, P)) * 0.45),
            "task_mats": bf(np.random.standard_normal((P, D, D)) / np.sqrt(D) / s[None, :, None] * s[None, None, :])}


def reference(transformed, coeff, task_mats):
    x, c, m = f64(transformed), f64(coeff), f64(task_mats)
    for j in range(P):
        x = x + c[:, j:j + 1] * (mxq(x, 1, "e4m3") @ mxq(m[j], 0, "e4m3"))
    return x

@@ -1,0 +1,179 @@
+from contextlib import ExitStack
+
+import concourse.mybir as mybir
+from concourse.masks import make_identity
+
+F32 = mybir.dt.float32
+BF16 = mybir.dt.bfloat16
+U32 = mybir.dt.uint32
+U8 = mybir.dt.uint8
+FP8X4 = mybir.dt.float8_e4m3fn_x4
+MULT = mybir.AluOpType.mult
+ADD = mybir.AluOpType.add
+
+P = 128
+PACK = 4
+K_PASS = P * PACK
+D = 1024
+STEPS = 2
+PASSES = D // K_PASS
+HALF = 512
+HALVES = D // HALF
+RUN = 4
+
+SCALAR_COLS = 256
+
+QUANTISE_LAG = 1
+SUM_LAG = 2
+COPY_LAG = 3
+FEATURES_LAG = 4
+
+FLOPS = 2 * STEPS * P * D * D
+
+
+def tile_precomputedmetanet_pa_s_kernel(tc, transformed, coeff, task_mats, out):
+    nc = tc.nc
+    with ExitStack() as ctx:
+        keep = ctx.enter_context(tc.tile_pool(name="keep", bufs=1))
+        stage = ctx.enter_context(tc.tile_pool(name="stage", bufs=3))
+        psum = ctx.enter_context(tc.psum_pool(name="psum", bufs=1))
+        ctx.enter_context(tc.manual_schedule())
+
+        x_sb = keep.tile([P, D], BF16)
+        nc.scalar.dma_start(out=x_sb[:], in_=transformed)
+        coeff_bf = keep.tile([P, STEPS], BF16)
+        nc.scalar.dma_start(out=coeff_bf[:], in_=coeff)
+
+        raw = [
+            [keep.tile([P, PACK, D], BF16, name="raw_%d_%d" % (j, g)) for g in range(PASSES)]
+            for j in range(STEPS)
+        ]
+        by_k = task_mats.rearrange("j (g p t) n -> j g p t n", g=PASSES, p=P, t=PACK)
+        for h in range(HALVES):
+            for u in range(2):
+                nc.sync.dma_start(
+                    out=raw[0][0][:, 2 * u : 2 * u + 2, h * HALF : (h + 1) * HALF],
+                    in_=by_k[0, 0, :, 2 * u : 2 * u + 2, h * HALF : (h + 1) * HALF],
+                )
+        for j in range(STEPS):
+            for g in range(PASSES):
+                if (j, g) != (0, 0):
+                    nc.sync.dma_start(out=raw[j][g][:], in_=by_k[j, g])
+
+        ident = keep.tile([P, P], F32)
+        make_identity(nc, ident[:])
+        coeff_f32 = keep.tile([P, STEPS], F32)
+        nc.gpsimd.tensor_copy(out=coeff_f32[:], in_=coeff_bf[:])
+
+        m_codes = [
+            [keep.tile([P, D], U32, align_bytes=64, name="m_codes_%d_%d" % (j, g)) for g in range(PASSES)]
+            for j in range(STEPS)
+        ]
+        m_scales = [
+            [keep.tile([P, D], U8, align_bytes=64, name="m_scales_%d_%d" % (j, g)) for g in range(PASSES)]
+            for j in range(STEPS)
+        ]
+        f_grouped = [keep.tile([P, PASSES * P * PACK], BF16, align_bytes=64, name="f_grouped_%d" % j) for j in range(STEPS)]
+        f_codes = [keep.tile([P, PASSES * P], U32, align_bytes=64, name="f_codes_%d" % j) for j in range(STEPS)]
+        f_scales = [keep.tile([P, PASSES * P], U8, align_bytes=64, name="f_scales_%d" % j) for j in range(STEPS)]
+
+        x1 = keep.tile([P, D], F32)
+        result = keep.tile([P, D], F32)
+        y = [
+            [psum.tile([P, HALF], F32, name="y_%d_%d" % (j, h)) for h in range(HALVES)]
+            for j in range(STEPS)
+        ]
+
+        x1_t = [psum.tile([P, PACK, P], F32, name="x1_t_%d" % h) for h in range(HALVES)]
+        grouped = {}
+
+        def regroup(j, g, h):
+            tile_ = stage.tile([P, HALF, PACK], BF16, align_bytes=64, name="grouped")
+            first = h * HALF
+            nc.scalar.copy(
+                out=tile_[:, :SCALAR_COLS, :].rearrange("p (c i) t -> p c t i", i=RUN),
+                in_=raw[j][g][:, :, first : first + SCALAR_COLS].rearrange("p t (c i) -> p c t i", i=RUN),
+            )
+            nc.vector.tensor_copy(
+                out=tile_[:, SCALAR_COLS:, :].rearrange("p (c i) t -> p c t i", i=RUN),
+                in_=raw[j][g][:, :, first + SCALAR_COLS : first + HALF].rearrange("p t (c i) -> p c t i", i=RUN),
+            )
+            grouped[(j, g, h)] = tile_
+
+        def quantise_and_multiply(j, g, h):
+            cols = slice(h * HALF, (h + 1) * HALF)
+            nc.vector.quantize_mx(
+                out=m_codes[j][g][:, cols].bitcast(FP8X4),
+                scales=m_scales[j][g][:, cols],
+                in_=grouped[(j, g, h)][:].rearrange("p c t -> p (c t)"),
+            )
+            if g == PASSES - 1:
+                for c in range(PASSES):
+                    samples = slice(c * P, (c + 1) * P)
+                    nc.tensor.matmul_mx(
+                        out=y[j][h][:],
+                        lhsT=f_codes[j][:, samples].bitcast(FP8X4),
+                        lhsT_scale=f_scales[j][:, samples],
+                        rhs=m_codes[j][c][:, cols].bitcast(FP8X4),
+                        rhs_scale=m_scales[j][c][:, cols],
+                        start=(c == 0),
+                        stop=(c == PASSES - 1),
+                    )
+
+        def quantise_features(j, first_pass, end_pass):
+            nc.vector.quantize_mx(
+                out=f_codes[j][:, first_pass * P : end_pass * P].bitcast(FP8X4),
+                scales=f_scales[j][:, first_pass * P : end_pass * P],
+                in_=f_grouped[j][:, first_pass * K_PASS : end_pass * K_PASS],
+            )
+
+        def add_residual(j, g, h):
+            cols = slice(h * HALF, (h + 1) * HALF)
+            if g == PASSES - 1 and j == 0:
+                nc.vector.scalar_tensor_tensor(
+                    out=x1[:, cols], in0=y[0][h][:], scalar=coeff_f32[:, 0:1], in1=x_sb[:, cols],
+                    op0=MULT, op1=ADD,
+                )
+                x1_by_k = x1[:].rearrange("s (g p t) -> s g t p", g=PASSES, p=P, t=PACK)
+                for t in range(PACK):
+                    nc.tensor.transpose(x1_t[h][:, t, :], x1_by_k[:, h, t, :], ident[:])
+            if g == PASSES - 1 and j == 1:
+                nc.vector.scalar_tensor_tensor(
+                    out=result[:, cols], in0=y[1][h][:], scalar=coeff_f32[:, 1:2], in1=x1[:, cols],
+                    op0=MULT, op1=ADD,
+                )
+                nc.sync.dma_start(out=out[:, cols], in_=result[:, cols])
+
+        def round_x1(j, g, h):
+            if g == PASSES - 1 and j == 0:
+                nc.scalar.copy(
+                    out=f_grouped[1][:, h * K_PASS : (h + 1) * K_PASS].rearrange("p (s t) -> p s t", t=PACK),
+                    in_=x1_t[h][:].rearrange("p t s -> p s t"),
+                )
+
+        def quantise_x1(j, g, h):
+            if g == PASSES - 1 and j == 0:
+                quantise_features(1, h, h + 1)
+
+        x_words = x_sb[:].bitcast(F32).rearrange("s (g p u) -> s g u p", g=PASSES, p=P, u=2)
+        x_t = psum.tile([P, PASSES * 2, P], F32)
+        for b in range(PASSES * 2):
+            nc.tensor.transpose(x_t[:, b, :], x_words[:, b // 2, b % 2, :], ident[:])
+        nc.scalar.copy(
+            out=f_grouped[0][:].bitcast(F32).rearrange("p (g s u) -> p g s u", g=PASSES, u=2),
+            in_=x_t[:].rearrange("p (g u) s -> p g s u", u=2),
+        )
+        quantise_features(0, 0, PASSES)
+
+        chunks = [(j, g, h) for j in range(STEPS) for g in range(PASSES) for h in range(HALVES)]
+
+        def at(stage_of_pipeline, i):
+            if 0 <= i < len(chunks):
+                stage_of_pipeline(*chunks[i])
+
+        for i in range(len(chunks) + FEATURES_LAG):
+            at(regroup, i)
+            at(quantise_x1, i - FEATURES_LAG)
+            at(quantise_and_multiply, i - QUANTISE_LAG)
+            at(add_residual, i - SUM_LAG)
+            at(round_x1, i - COPY_LAG)

@@ -21,12 +21,20 @@ HALF = 512
 HALVES = D // HALF
 RUN = 4
 
-SCALAR_COLS = 256
-
-QUANTISE_LAG = 1
-SUM_LAG = 2
-COPY_LAG = 3
-FEATURES_LAG = 4
+HALF_UNIT = HALF // 2
+UNITS = [
+    (0, 0, 0, HALF_UNIT),
+    (0, 0, HALF_UNIT, HALF_UNIT),
+    (0, 0, HALF, HALF),
+    (0, 1, 0, HALF),
+    (0, 1, HALF, HALF),
+    (1, 0, 0, HALF),
+    (1, 0, HALF, HALF),
+    (1, 1, 0, HALF),
+    (1, 1, HALF, HALF_UNIT),
+    (1, 1, HALF + HALF_UNIT, HALF_UNIT),
+]
+SCALAR_SIXTEENTHS = 8
 
 FLOPS = 2 * STEPS * P * D * D
 
@@ -35,35 +43,38 @@ def tile_precomputedmetanet_pa_s_kernel(tc, transformed, coeff, task_mats, out):
     nc = tc.nc
     with ExitStack() as ctx:
         keep = ctx.enter_context(tc.tile_pool(name="keep", bufs=1))
-        stage = ctx.enter_context(tc.tile_pool(name="stage", bufs=3))
+        stage = ctx.enter_context(tc.tile_pool(name="stage", bufs=4))
         psum = ctx.enter_context(tc.psum_pool(name="psum", bufs=1))
         ctx.enter_context(tc.manual_schedule())
 
         x_sb = keep.tile([P, D], BF16)
-        nc.scalar.dma_start(out=x_sb[:], in_=transformed)
-        coeff_bf = keep.tile([P, STEPS], BF16)
-        nc.scalar.dma_start(out=coeff_bf[:], in_=coeff)
-
-        raw = [
-            [keep.tile([P, PACK, D], BF16, name="raw_%d_%d" % (j, g)) for g in range(PASSES)]
-            for j in range(STEPS)
-        ]
+        coeff_sb = keep.tile([P, STEPS], BF16)
         by_k = task_mats.rearrange("j (g p t) n -> j g p t n", g=PASSES, p=P, t=PACK)
-        for h in range(HALVES):
-            for u in range(2):
-                nc.sync.dma_start(
-                    out=raw[0][0][:, 2 * u : 2 * u + 2, h * HALF : (h + 1) * HALF],
-                    in_=by_k[0, 0, :, 2 * u : 2 * u + 2, h * HALF : (h + 1) * HALF],
-                )
-        for j in range(STEPS):
-            for g in range(PASSES):
-                if (j, g) != (0, 0):
-                    nc.sync.dma_start(out=raw[j][g][:], in_=by_k[j, g])
+        raw = {}
+
+        def load(j, g, first, width):
+            tile_ = keep.tile([P, PACK, width], BF16, name="raw_%d_%d_%d" % (j, g, first))
+            nc.sync.dma_start(out=tile_[:], in_=by_k[j, g, :, :, first : first + width])
+            for i, (uj, ug, ufirst, uwidth) in enumerate(UNITS):
+                if (uj, ug) == (j, g) and first <= ufirst and ufirst + uwidth <= first + width:
+                    raw[i] = tile_[:, :, ufirst - first : ufirst - first + uwidth]
+
+        load(0, 0, 0, HALF_UNIT)
+        load(0, 0, HALF_UNIT, HALF_UNIT)
+        nc.scalar.dma_start(out=coeff_sb[:], in_=coeff)
+        load(0, 0, HALF, HALF)
+        nc.sync.dma_start(out=x_sb[:], in_=transformed)
+        load(0, 1, 0, HALF)
+        load(0, 1, HALF, HALF)
+        load(1, 0, 0, D)
+        load(1, 1, 0, D)
+
+        spark = keep.tile([P, 2], F32)
+        nc.vector.memset(spark[:, 0:1], 0.0)
+        nc.scalar.copy(out=spark[:, 1:2], in_=spark[:, 0:1])
 
         ident = keep.tile([P, P], F32)
         make_identity(nc, ident[:])
-        coeff_f32 = keep.tile([P, STEPS], F32)
-        nc.gpsimd.tensor_copy(out=coeff_f32[:], in_=coeff_bf[:])
 
         m_codes = [
             [keep.tile([P, D], U32, align_bytes=64, name="m_codes_%d_%d" % (j, g)) for g in range(PASSES)]
@@ -79,46 +90,49 @@ def tile_precomputedmetanet_pa_s_kernel(tc, transformed, coeff, task_mats, out):
 
         x1 = keep.tile([P, D], F32)
         result = keep.tile([P, D], F32)
-        y = [
-            [psum.tile([P, HALF], F32, name="y_%d_%d" % (j, h)) for h in range(HALVES)]
-            for j in range(STEPS)
-        ]
-
+        y = {
+            (j, first): psum.tile([P, HALF], F32, name="y_%d_%d" % (j, first))
+            for (j, first) in ((0, 0), (0, HALF), (1, 0), (1, HALF), (1, HALF + HALF_UNIT))
+        }
         x1_t = [psum.tile([P, PACK, P], F32, name="x1_t_%d" % h) for h in range(HALVES)]
+        x_t = psum.tile([P, PASSES * 2, P], F32)
         grouped = {}
 
-        def regroup(j, g, h):
+        def regroup(i):
+            j, g, first, width = UNITS[i]
+            split = width * SCALAR_SIXTEENTHS // 16
             tile_ = stage.tile([P, HALF, PACK], BF16, align_bytes=64, name="grouped")
-            first = h * HALF
             nc.scalar.copy(
-                out=tile_[:, :SCALAR_COLS, :].rearrange("p (c i) t -> p c t i", i=RUN),
-                in_=raw[j][g][:, :, first : first + SCALAR_COLS].rearrange("p t (c i) -> p c t i", i=RUN),
+                out=tile_[:, :split, :].rearrange("p (c i) t -> p c t i", i=RUN),
+                in_=raw[i][:, :, :split].rearrange("p t (c i) -> p c t i", i=RUN),
             )
             nc.vector.tensor_copy(
-                out=tile_[:, SCALAR_COLS:, :].rearrange("p (c i) t -> p c t i", i=RUN),
-                in_=raw[j][g][:, :, first + SCALAR_COLS : first + HALF].rearrange("p t (c i) -> p c t i", i=RUN),
+                out=tile_[:, split:width, :].rearrange("p (c i) t -> p c t i", i=RUN),
+                in_=raw[i][:, :, split:].rearrange("p t (c i) -> p c t i", i=RUN),
             )
-            grouped[(j, g, h)] = tile_
+            grouped[i] = tile_
 
-        def quantise_and_multiply(j, g, h):
-            cols = slice(h * HALF, (h + 1) * HALF)
+        def quantise(i):
+            j, g, first, width = UNITS[i]
+            cols = slice(first, first + width)
             nc.vector.quantize_mx(
                 out=m_codes[j][g][:, cols].bitcast(FP8X4),
                 scales=m_scales[j][g][:, cols],
-                in_=grouped[(j, g, h)][:].rearrange("p c t -> p (c t)"),
+                in_=grouped[i][:, :width, :].rearrange("p c t -> p (c t)"),
             )
-            if g == PASSES - 1:
-                for c in range(PASSES):
-                    samples = slice(c * P, (c + 1) * P)
-                    nc.tensor.matmul_mx(
-                        out=y[j][h][:],
-                        lhsT=f_codes[j][:, samples].bitcast(FP8X4),
-                        lhsT_scale=f_scales[j][:, samples],
-                        rhs=m_codes[j][c][:, cols].bitcast(FP8X4),
-                        rhs_scale=m_scales[j][c][:, cols],
-                        start=(c == 0),
-                        stop=(c == PASSES - 1),
-                    )
+
+        def multiply(j, g, first, width):
+            samples = slice(g * P, (g + 1) * P)
+            cols = slice(first, first + width)
+            nc.tensor.matmul_mx(
+                out=y[(j, first)][:, :width],
+                lhsT=f_codes[j][:, samples].bitcast(FP8X4),
+                lhsT_scale=f_scales[j][:, samples],
+                rhs=m_codes[j][g][:, cols].bitcast(FP8X4),
+                rhs_scale=m_scales[j][g][:, cols],
+                start=(g == 0),
+                stop=(g == PASSES - 1),
+            )
 
         def quantise_features(j, first_pass, end_pass):
             nc.vector.quantize_mx(
@@ -127,53 +141,77 @@ def tile_precomputedmetanet_pa_s_kernel(tc, transformed, coeff, task_mats, out):
                 in_=f_grouped[j][:, first_pass * K_PASS : end_pass * K_PASS],
             )
 
-        def add_residual(j, g, h):
+        def transpose_x():
+            x_words = x_sb[:].bitcast(F32).rearrange("s (g p u) -> s g u p", g=PASSES, p=P, u=2)
+            for b in range(PASSES * 2):
+                nc.tensor.transpose(x_t[:, b, :], x_words[:, b // 2, b % 2, :], ident[:])
+            nc.scalar.copy(
+                out=f_grouped[0][:].bitcast(F32).rearrange("p (g s u) -> p g s u", g=PASSES, u=2),
+                in_=x_t[:].rearrange("p (g u) s -> p g s u", u=2),
+            )
+
+        def make_x1(h):
             cols = slice(h * HALF, (h + 1) * HALF)
-            if g == PASSES - 1 and j == 0:
-                nc.vector.scalar_tensor_tensor(
-                    out=x1[:, cols], in0=y[0][h][:], scalar=coeff_f32[:, 0:1], in1=x_sb[:, cols],
-                    op0=MULT, op1=ADD,
-                )
-                x1_by_k = x1[:].rearrange("s (g p t) -> s g t p", g=PASSES, p=P, t=PACK)
-                for t in range(PACK):
-                    nc.tensor.transpose(x1_t[h][:, t, :], x1_by_k[:, h, t, :], ident[:])
-            if g == PASSES - 1 and j == 1:
-                nc.vector.scalar_tensor_tensor(
-                    out=result[:, cols], in0=y[1][h][:], scalar=coeff_f32[:, 1:2], in1=x1[:, cols],
-                    op0=MULT, op1=ADD,
-                )
-                nc.sync.dma_start(out=out[:, cols], in_=result[:, cols])
+            nc.vector.scalar_tensor_tensor(
+                out=x1[:, cols], in0=y[(0, h * HALF)][:], scalar=coeff_sb[:, 0:1], in1=x_sb[:, cols],
+                op0=MULT, op1=ADD,
+            )
+            x1_by_k = x1[:].rearrange("s (g p t) -> s g t p", g=PASSES, p=P, t=PACK)
+            for t in range(PACK):
+                nc.tensor.transpose(x1_t[h][:, t, :], x1_by_k[:, h, t, :], ident[:])
 
-        def round_x1(j, g, h):
-            if g == PASSES - 1 and j == 0:
-                nc.scalar.copy(
-                    out=f_grouped[1][:, h * K_PASS : (h + 1) * K_PASS].rearrange("p (s t) -> p s t", t=PACK),
-                    in_=x1_t[h][:].rearrange("p t s -> p s t"),
-                )
+        def round_x1(h):
+            nc.scalar.copy(
+                out=f_grouped[1][:, h * K_PASS : (h + 1) * K_PASS].rearrange("p (s t) -> p s t", t=PACK),
+                in_=x1_t[h][:].rearrange("p t s -> p s t"),
+            )
 
-        def quantise_x1(j, g, h):
-            if g == PASSES - 1 and j == 0:
-                quantise_features(1, h, h + 1)
+        def make_out(first, width, queue):
+            cols = slice(first, first + width)
+            nc.vector.scalar_tensor_tensor(
+                out=result[:, cols], in0=y[(1, first)][:, :width], scalar=coeff_sb[:, 1:2], in1=x1[:, cols],
+                op0=MULT, op1=ADD,
+            )
+            queue.dma_start(out=out[:, cols], in_=result[:, cols])
 
-        x_words = x_sb[:].bitcast(F32).rearrange("s (g p u) -> s g u p", g=PASSES, p=P, u=2)
-        x_t = psum.tile([P, PASSES * 2, P], F32)
-        for b in range(PASSES * 2):
-            nc.tensor.transpose(x_t[:, b, :], x_words[:, b // 2, b % 2, :], ident[:])
-        nc.scalar.copy(
-            out=f_grouped[0][:].bitcast(F32).rearrange("p (g s u) -> p g s u", g=PASSES, u=2),
-            in_=x_t[:].rearrange("p (g u) s -> p g s u", u=2),
-        )
+        regroup(0)
+        regroup(1)
+        quantise(0)
+        regroup(2)
+        transpose_x()
+        quantise(1)
+        regroup(3)
         quantise_features(0, 0, PASSES)
-
-        chunks = [(j, g, h) for j in range(STEPS) for g in range(PASSES) for h in range(HALVES)]
-
-        def at(stage_of_pipeline, i):
-            if 0 <= i < len(chunks):
-                stage_of_pipeline(*chunks[i])
-
-        for i in range(len(chunks) + FEATURES_LAG):
-            at(regroup, i)
-            at(quantise_x1, i - FEATURES_LAG)
-            at(quantise_and_multiply, i - QUANTISE_LAG)
-            at(add_residual, i - SUM_LAG)
-            at(round_x1, i - COPY_LAG)
+        quantise(2)
+        multiply(0, 0, 0, HALF)
+        multiply(0, 0, HALF, HALF)
+        regroup(4)
+        quantise(3)
+        multiply(0, 1, 0, HALF)
+        regroup(5)
+        quantise(4)
+        multiply(0, 1, HALF, HALF)
+        make_x1(0)
+        regroup(6)
+        round_x1(0)
+        quantise(5)
+        make_x1(1)
+        regroup(7)
+        round_x1(1)
+        quantise_features(1, 0, 1)
+        quantise(6)
+        multiply(1, 0, 0, HALF)
+        multiply(1, 0, HALF, HALF_UNIT)
+        multiply(1, 0, HALF + HALF_UNIT, HALF_UNIT)
+        regroup(8)
+        quantise_features(1, 1, 2)
+        quantise(7)
+        multiply(1, 1, 0, HALF)
+        regroup(9)
+        make_out(0, HALF, nc.sync)
+        quantise(8)
+        multiply(1, 1, HALF, HALF_UNIT)
+        quantise(9)
+        multiply(1, 1, HALF + HALF_UNIT, HALF_UNIT)
+        make_out(HALF, HALF_UNIT, nc.sync)
+        make_out(HALF + HALF_UNIT, HALF_UNIT, nc.scalar)

@@ -204,13 +204,13 @@ def tile_precomputedmetanet_pa_s_kernel(tc, transformed, coeff, task_mats, out):
         multiply(1, 0, HALF, HALF_UNIT)
         multiply(1, 0, HALF + HALF_UNIT, HALF_UNIT)
         regroup(8)
-        quantise_features(1, 1, 2)
         quantise(7)
+        quantise_features(1, 1, 2)
         multiply(1, 1, 0, HALF)
         regroup(9)
-        make_out(0, HALF, nc.sync)
         quantise(8)
         multiply(1, 1, HALF, HALF_UNIT)
+        make_out(0, HALF, nc.sync)
         quantise(9)
         multiply(1, 1, HALF + HALF_UNIT, HALF_UNIT)
         make_out(HALF, HALF_UNIT, nc.sync)

@@ -194,8 +194,8 @@ def tile_precomputedmetanet_pa_s_kernel(tc, transformed, coeff, task_mats, out):
         make_x1(0)
         regroup(6)
         round_x1(0)
-        quantise(5)
         make_x1(1)
+        quantise(5)
         regroup(7)
         round_x1(1)
         quantise_features(1, 0, 1)

@@ -34,7 +34,7 @@ UNITS = [
     (1, 1, HALF, HALF_UNIT),
     (1, 1, HALF + HALF_UNIT, HALF_UNIT),
 ]
-SCALAR_SIXTEENTHS = 8
+SCALAR_SIXTEENTHS = 9
 
 FLOPS = 2 * STEPS * P * D * D
 
@@ -59,14 +59,14 @@ def tile_precomputedmetanet_pa_s_kernel(tc, transformed, coeff, task_mats, out):
                 if (uj, ug) == (j, g) and first <= ufirst and ufirst + uwidth <= first + width:
                     raw[i] = tile_[:, :, ufirst - first : ufirst - first + uwidth]
 
-        load(0, 0, 0, HALF_UNIT)
-        load(0, 0, HALF_UNIT, HALF_UNIT)
+        load(0, 0, 0, HALF)
         nc.scalar.dma_start(out=coeff_sb[:], in_=coeff)
         load(0, 0, HALF, HALF)
         nc.sync.dma_start(out=x_sb[:], in_=transformed)
         load(0, 1, 0, HALF)
         load(0, 1, HALF, HALF)
-        load(1, 0, 0, D)
+        load(1, 0, 0, HALF)
+        load(1, 0, HALF, HALF)
         load(1, 1, 0, D)
 
         spark = keep.tile([P, 2], F32)

@@ -23,8 +23,7 @@ RUN = 4
 
 HALF_UNIT = HALF // 2
 UNITS = [
-    (0, 0, 0, HALF_UNIT),
-    (0, 0, HALF_UNIT, HALF_UNIT),
+    (0, 0, 0, HALF),
     (0, 0, HALF, HALF),
     (0, 1, 0, HALF),
     (0, 1, HALF, HALF),
@@ -67,7 +66,8 @@ def tile_precomputedmetanet_pa_s_kernel(tc, transformed, coeff, task_mats, out):
         load(0, 1, HALF, HALF)
         load(1, 0, 0, HALF)
         load(1, 0, HALF, HALF)
-        load(1, 1, 0, D)
+        load(1, 1, 0, HALF)
+        load(1, 1, HALF, HALF)
 
         spark = keep.tile([P, 2], F32)
         nc.vector.memset(spark[:, 0:1], 0.0)
@@ -166,10 +166,11 @@ def tile_precomputedmetanet_pa_s_kernel(tc, transformed, coeff, task_mats, out):
                 in_=x1_t[h][:].rearrange("p t s -> p s t"),
             )
 
-        def make_out(first, width, queue):
+        def make_out(bank, first, width, queue):
             cols = slice(first, first + width)
             nc.vector.scalar_tensor_tensor(
-                out=result[:, cols], in0=y[(1, first)][:, :width], scalar=coeff_sb[:, 1:2], in1=x1[:, cols],
+                out=result[:, cols], in0=y[(1, bank)][:, first - bank : first - bank + width],
+                scalar=coeff_sb[:, 1:2], in1=x1[:, cols],
                 op0=MULT, op1=ADD,
             )
             queue.dma_start(out=out[:, cols], in_=result[:, cols])
@@ -177,41 +178,40 @@ def tile_precomputedmetanet_pa_s_kernel(tc, transformed, coeff, task_mats, out):
         regroup(0)
         regroup(1)
         quantise(0)
-        regroup(2)
         transpose_x()
-        quantise(1)
-        regroup(3)
+        regroup(2)
         quantise_features(0, 0, PASSES)
-        quantise(2)
+        quantise(1)
         multiply(0, 0, 0, HALF)
         multiply(0, 0, HALF, HALF)
+        regroup(3)
+        quantise(2)
+        multiply(0, 1, 0, HALF)
         regroup(4)
         quantise(3)
-        multiply(0, 1, 0, HALF)
-        regroup(5)
-        quantise(4)
         multiply(0, 1, HALF, HALF)
         make_x1(0)
+        regroup(5)
+        make_x1(1)
+        quantise(4)
         regroup(6)
         round_x1(0)
-        make_x1(1)
-        quantise(5)
-        regroup(7)
         round_x1(1)
+        quantise(5)
         quantise_features(1, 0, 1)
-        quantise(6)
         multiply(1, 0, 0, HALF)
         multiply(1, 0, HALF, HALF_UNIT)
         multiply(1, 0, HALF + HALF_UNIT, HALF_UNIT)
-        regroup(8)
-        quantise(7)
+        regroup(7)
+        quantise(6)
         quantise_features(1, 1, 2)
         multiply(1, 1, 0, HALF)
-        regroup(9)
-        quantise(8)
+        regroup(8)
+        quantise(7)
         multiply(1, 1, HALF, HALF_UNIT)
-        make_out(0, HALF, nc.sync)
-        quantise(9)
+        quantise(8)
         multiply(1, 1, HALF + HALF_UNIT, HALF_UNIT)
-        make_out(HALF, HALF_UNIT, nc.sync)
-        make_out(HALF + HALF_UNIT, HALF_UNIT, nc.scalar)
+        make_out(0, 0, HALF_UNIT, nc.sync)
+        make_out(0, HALF_UNIT, HALF_UNIT, nc.scalar)
+        make_out(HALF, HALF, HALF_UNIT, nc.sync)
+        make_out(HALF + HALF_UNIT, HALF + HALF_UNIT, HALF_UNIT, nc.scalar)

@@ -33,7 +33,7 @@ UNITS = [
     (1, 1, HALF, HALF_UNIT),
     (1, 1, HALF + HALF_UNIT, HALF_UNIT),
 ]
-SCALAR_SIXTEENTHS = 9
+SCALAR_SIXTEENTHS = 8
 
 FLOPS = 2 * STEPS * P * D * D
 
@@ -58,10 +58,10 @@ def tile_precomputedmetanet_pa_s_kernel(tc, transformed, coeff, task_mats, out):
                 if (uj, ug) == (j, g) and first <= ufirst and ufirst + uwidth <= first + width:
                     raw[i] = tile_[:, :, ufirst - first : ufirst - first + uwidth]
 
-        load(0, 0, 0, HALF)
-        nc.scalar.dma_start(out=coeff_sb[:], in_=coeff)
-        load(0, 0, HALF, HALF)
         nc.sync.dma_start(out=x_sb[:], in_=transformed)
+        nc.scalar.dma_start(out=coeff_sb[:], in_=coeff)
+        load(0, 0, 0, HALF)
+        load(0, 0, HALF, HALF)
         load(0, 1, 0, HALF)
         load(0, 1, HALF, HALF)
         load(1, 0, 0, HALF)
@@ -166,23 +166,25 @@ def tile_precomputedmetanet_pa_s_kernel(tc, transformed, coeff, task_mats, out):
                 in_=x1_t[h][:].rearrange("p t s -> p s t"),
             )
 
-        def make_out(bank, first, width, queue):
+        def make_out(first, width):
             cols = slice(first, first + width)
             nc.vector.scalar_tensor_tensor(
-                out=result[:, cols], in0=y[(1, bank)][:, first - bank : first - bank + width],
-                scalar=coeff_sb[:, 1:2], in1=x1[:, cols],
+                out=result[:, cols], in0=y[(1, first)][:, :width], scalar=coeff_sb[:, 1:2], in1=x1[:, cols],
                 op0=MULT, op1=ADD,
             )
+
+        def store(h, queue):
+            cols = slice(h * HALF, (h + 1) * HALF)
             queue.dma_start(out=out[:, cols], in_=result[:, cols])
 
+        transpose_x()
         regroup(0)
+        quantise_features(0, 0, PASSES)
         regroup(1)
         quantise(0)
-        transpose_x()
-        regroup(2)
-        quantise_features(0, 0, PASSES)
-        quantise(1)
         multiply(0, 0, 0, HALF)
+        regroup(2)
+        quantise(1)
         multiply(0, 0, HALF, HALF)
         regroup(3)
         quantise(2)
@@ -211,7 +213,8 @@ def tile_precomputedmetanet_pa_s_kernel(tc, transformed, coeff, task_mats, out):
         multiply(1, 1, HALF, HALF_UNIT)
         quantise(8)
         multiply(1, 1, HALF + HALF_UNIT, HALF_UNIT)
-        make_out(0, 0, HALF_UNIT, nc.sync)
-        make_out(0, HALF_UNIT, HALF_UNIT, nc.scalar)
-        make_out(HALF, HALF, HALF_UNIT, nc.sync)
-        make_out(HALF + HALF_UNIT, HALF + HALF_UNIT, HALF_UNIT, nc.scalar)
+        make_out(0, HALF)
+        store(0, nc.sync)
+        make_out(HALF, HALF_UNIT)
+        make_out(HALF + HALF_UNIT, HALF_UNIT)
+        store(1, nc.scalar)

@@ -23,17 +23,17 @@ RUN = 4
 
 HALF_UNIT = HALF // 2
 UNITS = [
-    (0, 0, 0, HALF),
-    (0, 0, HALF, HALF),
-    (0, 1, 0, HALF),
-    (0, 1, HALF, HALF),
-    (1, 0, 0, HALF),
-    (1, 0, HALF, HALF),
-    (1, 1, 0, HALF),
-    (1, 1, HALF, HALF_UNIT),
-    (1, 1, HALF + HALF_UNIT, HALF_UNIT),
+    (0, 0, 0, HALF, 8),
+    (0, 0, HALF, HALF, 8),
+    (0, 1, 0, HALF, 8),
+    (0, 1, HALF, HALF, 10),
+    (1, 0, 0, HALF, 10),
+    (1, 0, HALF, HALF, 10),
+    (1, 1, 0, HALF, 8),
+    (1, 1, HALF, HALF_UNIT, 8),
+    (1, 1, HALF + HALF_UNIT, HALF_UNIT, 6),
 ]
-SCALAR_SIXTEENTHS = 8
+SIXTEENTHS = 16
 
 FLOPS = 2 * STEPS * P * D * D
 
@@ -54,7 +54,7 @@ def tile_precomputedmetanet_pa_s_kernel(tc, transformed, coeff, task_mats, out):
         def load(j, g, first, width):
             tile_ = keep.tile([P, PACK, width], BF16, name="raw_%d_%d_%d" % (j, g, first))
             nc.sync.dma_start(out=tile_[:], in_=by_k[j, g, :, :, first : first + width])
-            for i, (uj, ug, ufirst, uwidth) in enumerate(UNITS):
+            for i, (uj, ug, ufirst, uwidth, share) in enumerate(UNITS):
                 if (uj, ug) == (j, g) and first <= ufirst and ufirst + uwidth <= first + width:
                     raw[i] = tile_[:, :, ufirst - first : ufirst - first + uwidth]
 
@@ -99,8 +99,8 @@ def tile_precomputedmetanet_pa_s_kernel(tc, transformed, coeff, task_mats, out):
         grouped = {}
 
         def regroup(i):
-            j, g, first, width = UNITS[i]
-            split = width * SCALAR_SIXTEENTHS // 16
+            j, g, first, width, share = UNITS[i]
+            split = width * share // SIXTEENTHS
             tile_ = stage.tile([P, HALF, PACK], BF16, align_bytes=64, name="grouped")
             nc.scalar.copy(
                 out=tile_[:, :split, :].rearrange("p (c i) t -> p c t i", i=RUN),
@@ -113,7 +113,7 @@ def tile_precomputedmetanet_pa_s_kernel(tc, transformed, coeff, task_mats, out):
             grouped[i] = tile_
 
         def quantise(i):
-            j, g, first, width = UNITS[i]
+            j, g, first, width, share = UNITS[i]
             cols = slice(first, first + width)
             nc.vector.quantize_mx(
                 out=m_codes[j][g][:, cols].bitcast(FP8X4),
@@ -194,10 +194,10 @@ def tile_precomputedmetanet_pa_s_kernel(tc, transformed, coeff, task_mats, out):
         multiply(0, 1, HALF, HALF)
         make_x1(0)
         regroup(5)
+        round_x1(0)
         make_x1(1)
         quantise(4)
         regroup(6)
-        round_x1(0)
         round_x1(1)
         quantise(5)
         quantise_features(1, 0, 1)

from contextlib import ExitStack

import concourse.mybir as mybir
from concourse.masks import make_identity

F32 = mybir.dt.float32
BF16 = mybir.dt.bfloat16
U32 = mybir.dt.uint32
U8 = mybir.dt.uint8
FP8X4 = mybir.dt.float8_e4m3fn_x4
MULT = mybir.AluOpType.mult
ADD = mybir.AluOpType.add

P = 128
PACK = 4
K_PASS = P * PACK
D = 1024
STEPS = 2
PASSES = D // K_PASS
HALF = 512
HALVES = D // HALF
RUN = 4

HALF_UNIT = HALF // 2
UNITS = [
    (0, 0, 0, HALF, 8),
    (0, 0, HALF, HALF, 8),
    (0, 1, 0, HALF, 8),
    (0, 1, HALF, HALF, 10),
    (1, 0, 0, HALF, 10),
    (1, 0, HALF, HALF, 10),
    (1, 1, 0, HALF, 8),
    (1, 1, HALF, HALF_UNIT, 8),
    (1, 1, HALF + HALF_UNIT, HALF_UNIT, 6),
]
SIXTEENTHS = 16

FLOPS = 2 * STEPS * P * D * D


def tile_precomputedmetanet_pa_s_kernel(tc, transformed, coeff, task_mats, out):
    nc = tc.nc
    with ExitStack() as ctx:
        keep = ctx.enter_context(tc.tile_pool(name="keep", bufs=1))
        stage = ctx.enter_context(tc.tile_pool(name="stage", bufs=4))
        psum = ctx.enter_context(tc.psum_pool(name="psum", bufs=1))
        ctx.enter_context(tc.manual_schedule())

        x_sb = keep.tile([P, D], BF16)
        coeff_sb = keep.tile([P, STEPS], BF16)
        by_k = task_mats.rearrange("j (g p t) n -> j g p t n", g=PASSES, p=P, t=PACK)
        raw = {}

        def load(j, g, first, width):
            tile_ = keep.tile([P, PACK, width], BF16, name="raw_%d_%d_%d" % (j, g, first))
            nc.sync.dma_start(out=tile_[:], in_=by_k[j, g, :, :, first : first + width])
            for i, (uj, ug, ufirst, uwidth, share) in enumerate(UNITS):
                if (uj, ug) == (j, g) and first <= ufirst and ufirst + uwidth <= first + width:
                    raw[i] = tile_[:, :, ufirst - first : ufirst - first + uwidth]

        nc.sync.dma_start(out=x_sb[:], in_=transformed)
        nc.scalar.dma_start(out=coeff_sb[:], in_=coeff)
        load(0, 0, 0, HALF)
        load(0, 0, HALF, HALF)
        load(0, 1, 0, HALF)
        load(0, 1, HALF, HALF)
        load(1, 0, 0, HALF)
        load(1, 0, HALF, HALF)
        load(1, 1, 0, HALF)
        load(1, 1, HALF, HALF)

        spark = keep.tile([P, 2], F32)
        nc.vector.memset(spark[:, 0:1], 0.0)
        nc.scalar.copy(out=spark[:, 1:2], in_=spark[:, 0:1])

        ident = keep.tile([P, P], F32)
        make_identity(nc, ident[:])

        m_codes = [
            [keep.tile([P, D], U32, align_bytes=64, name="m_codes_%d_%d" % (j, g)) for g in range(PASSES)]
            for j in range(STEPS)
        ]
        m_scales = [
            [keep.tile([P, D], U8, align_bytes=64, name="m_scales_%d_%d" % (j, g)) for g in range(PASSES)]
            for j in range(STEPS)
        ]
        f_grouped = [keep.tile([P, PASSES * P * PACK], BF16, align_bytes=64, name="f_grouped_%d" % j) for j in range(STEPS)]
        f_codes = [keep.tile([P, PASSES * P], U32, align_bytes=64, name="f_codes_%d" % j) for j in range(STEPS)]
        f_scales = [keep.tile([P, PASSES * P], U8, align_bytes=64, name="f_scales_%d" % j) for j in range(STEPS)]

        x1 = keep.tile([P, D], F32)
        result = keep.tile([P, D], F32)
        y = {
            (j, first): psum.tile([P, HALF], F32, name="y_%d_%d" % (j, first))
            for (j, first) in ((0, 0), (0, HALF), (1, 0), (1, HALF), (1, HALF + HALF_UNIT))
        }
        x1_t = [psum.tile([P, PACK, P], F32, name="x1_t_%d" % h) for h in range(HALVES)]
        x_t = psum.tile([P, PASSES * 2, P], F32)
        grouped = {}

        def regroup(i):
            j, g, first, width, share = UNITS[i]
            split = width * share // SIXTEENTHS
            tile_ = stage.tile([P, HALF, PACK], BF16, align_bytes=64, name="grouped")
            nc.scalar.copy(
                out=tile_[:, :split, :].rearrange("p (c i) t -> p c t i", i=RUN),
                in_=raw[i][:, :, :split].rearrange("p t (c i) -> p c t i", i=RUN),
            )
            nc.vector.tensor_copy(
                out=tile_[:, split:width, :].rearrange("p (c i) t -> p c t i", i=RUN),
                in_=raw[i][:, :, split:].rearrange("p t (c i) -> p c t i", i=RUN),
            )
            grouped[i] = tile_

        def quantise(i):
            j, g, first, width, share = UNITS[i]
            cols = slice(first, first + width)
            nc.vector.quantize_mx(
                out=m_codes[j][g][:, cols].bitcast(FP8X4),
                scales=m_scales[j][g][:, cols],
                in_=grouped[i][:, :width, :].rearrange("p c t -> p (c t)"),
            )

        def multiply(j, g, first, width):
            samples = slice(g * P, (g + 1) * P)
            cols = slice(first, first + width)
            nc.tensor.matmul_mx(
                out=y[(j, first)][:, :width],
                lhsT=f_codes[j][:, samples].bitcast(FP8X4),
                lhsT_scale=f_scales[j][:, samples],
                rhs=m_codes[j][g][:, cols].bitcast(FP8X4),
                rhs_scale=m_scales[j][g][:, cols],
                start=(g == 0),
                stop=(g == PASSES - 1),
            )

        def quantise_features(j, first_pass, end_pass):
            nc.vector.quantize_mx(
                out=f_codes[j][:, first_pass * P : end_pass * P].bitcast(FP8X4),
                scales=f_scales[j][:, first_pass * P : end_pass * P],
                in_=f_grouped[j][:, first_pass * K_PASS : end_pass * K_PASS],
            )

        def transpose_x():
            x_words = x_sb[:].bitcast(F32).rearrange("s (g p u) -> s g u p", g=PASSES, p=P, u=2)
            for b in range(PASSES * 2):
                nc.tensor.transpose(x_t[:, b, :], x_words[:, b // 2, b % 2, :], ident[:])
            nc.scalar.copy(
                out=f_grouped[0][:].bitcast(F32).rearrange("p (g s u) -> p g s u", g=PASSES, u=2),
                in_=x_t[:].rearrange("p (g u) s -> p g s u", u=2),
            )

        def make_x1(h):
            cols = slice(h * HALF, (h + 1) * HALF)
            nc.vector.scalar_tensor_tensor(
                out=x1[:, cols], in0=y[(0, h * HALF)][:], scalar=coeff_sb[:, 0:1], in1=x_sb[:, cols],
                op0=MULT, op1=ADD,
            )
            x1_by_k = x1[:].rearrange("s (g p t) -> s g t p", g=PASSES, p=P, t=PACK)
            for t in range(PACK):
                nc.tensor.transpose(x1_t[h][:, t, :], x1_by_k[:, h, t, :], ident[:])

        def round_x1(h):
            nc.scalar.copy(
                out=f_grouped[1][:, h * K_PASS : (h + 1) * K_PASS].rearrange("p (s t) -> p s t", t=PACK),
                in_=x1_t[h][:].rearrange("p t s -> p s t"),
            )

        def make_out(first, width):
            cols = slice(first, first + width)
            nc.vector.scalar_tensor_tensor(
                out=result[:, cols], in0=y[(1, first)][:, :width], scalar=coeff_sb[:, 1:2], in1=x1[:, cols],
                op0=MULT, op1=ADD,
            )

        def store(h, queue):
            cols = slice(h * HALF, (h + 1) * HALF)
            queue.dma_start(out=out[:, cols], in_=result[:, cols])

        transpose_x()
        regroup(0)
        quantise_features(0, 0, PASSES)
        regroup(1)
        quantise(0)
        multiply(0, 0, 0, HALF)
        regroup(2)
        quantise(1)
        multiply(0, 0, HALF, HALF)
        regroup(3)
        quantise(2)
        multiply(0, 1, 0, HALF)
        regroup(4)
        quantise(3)
        multiply(0, 1, HALF, HALF)
        make_x1(0)
        regroup(5)
        round_x1(0)
        make_x1(1)
        quantise(4)
        regroup(6)
        round_x1(1)
        quantise(5)
        quantise_features(1, 0, 1)
        multiply(1, 0, 0, HALF)
        multiply(1, 0, HALF, HALF_UNIT)
        multiply(1, 0, HALF + HALF_UNIT, HALF_UNIT)
        regroup(7)
        quantise(6)
        quantise_features(1, 1, 2)
        multiply(1, 1, 0, HALF)
        regroup(8)
        quantise(7)
        multiply(1, 1, HALF, HALF_UNIT)
        quantise(8)
        multiply(1, 1, HALF + HALF_UNIT, HALF_UNIT)
        make_out(0, HALF)
        store(0, nc.sync)
        make_out(HALF, HALF_UNIT)
        make_out(HALF + HALF_UNIT, HALF_UNIT)
        store(1, nc.scalar)
